import numpy as np
import ml_dtypes


def mxq(x, axis, fmt="e4m3"):
    dtype, down = {"e4m3": (ml_dtypes.float8_e4m3fn, 7), "e5m2": (ml_dtypes.float8_e5m2, 14)}[fmt]
    v = np.moveaxis(np.asarray(x, np.float32).astype(ml_dtypes.bfloat16).astype(np.float64), axis, -1)
    blocks = v.reshape(v.shape[:-1] + (-1, 32))
    amax = np.abs(blocks).max(-1, keepdims=True)
    byte = np.maximum(np.where(amax > 0, np.frexp(amax)[1] - 1 + 127, 0) - down, 1)
    scale = np.exp2(byte - 127.0)
    codes = (blocks / scale).astype(np.float32).astype(dtype).astype(np.float64)
    return np.moveaxis((codes * scale).reshape(v.shape), -1, axis)


WIDE = False


def mx_kscale(k):
    if not WIDE:
        return np.ones(k)
    levels = np.array([10, -10, 5, -5, 0])
    a = np.random.permutation(np.resize(levels, k // 512 * 4)).reshape(k // 512, 4)
    idx = np.arange(k)
    return np.exp2(a[idx // 512, idx % 128 // 32])


BF16 = ml_dtypes.bfloat16


def bf(x):
    return np.asarray(x, np.float32).astype(BF16)


def f64(x):
    return np.asarray(x).astype(np.float64)


B, T, C, H, W = 1, 1536, 1024, 8, 512
D = C // H
HALF = D // 2
ROPE_BASE = 10000.0


def rotate_half(u):
    return np.concatenate([-u[..., HALF:], u[..., :HALF]], axis=-1)


def setup_inputs():
    s = mx_kscale(C)
    start = np.random.randint(0, T)
    inv_freq = 1.0 / (ROPE_BASE ** (np.arange(0, D, 2) / D))
    freqs = np.outer(start + np.arange(T), inv_freq)
    emb = np.concatenate([freqs, freqs], axis=-1)
    return {"x": bf(np.random.standard_normal((B, T, C)) * s),
            "freqs_cos": bf(np.cos(emb)),
            "freqs_sin": bf(np.sin(emb)),
            "w_attn": bf(np.random.standard_normal((C, 3 * C)) * 1.25 / np.sqrt(C) / s[:, None])}


def reference(x, freqs_cos, freqs_sin, w_attn):
    qkv = mxq(f64(x), 2, "e4m3") @ mxq(f64(w_attn), 0, "e4m3")
    q, k, v = np.split(qkv, 3, axis=-1)
    q = q.reshape(B, T, H, D).transpose(0, 2, 1, 3)
    k = k.reshape(B, T, H, D).transpose(0, 2, 1, 3)
    v = v.reshape(B, T, H, D).transpose(0, 2, 1, 3)
    cos = f64(freqs_cos)[None, None, :, :]
    sin = f64(freqs_sin)[None, None, :, :]
    q_rot = q * cos + rotate_half(q) * sin
    k_rot = k * cos + rotate_half(k) * sin
    return q_rot, k_rot, v

@@ -1,0 +1,230 @@
+from contextlib import ExitStack
+
+import concourse.mybir as mybir
+from concourse.masks import make_identity
+
+BF16 = mybir.dt.bfloat16
+F32 = mybir.dt.float32
+U32 = mybir.dt.uint32
+U8 = mybir.dt.uint8
+FP8X4 = mybir.dt.float8_e4m3fn_x4
+MULT = mybir.AluOpType.mult
+ADD = mybir.AluOpType.add
+
+P = 128
+T = 1536
+C = 1024
+D = 128
+HALF = D // 2
+TILES = T // P
+PACK = 4
+PASSES = C // (P * PACK)
+CHUNK = 512
+CHUNK_HEADS = CHUNK // D
+PIECE = 2
+STORE_TILES = 6
+
+FLOPS = 2 * T * C * 3 * C
+
+ROUNDS = (((0, 0),), ((1, 0), (2, 0)), ((0, 1), (2, 1)), ((1, 1),))
+V_THIRD = 2
+
+
+def tile_swaattention_pa_kernel(
+    tc, x, freqs_cos, freqs_sin, w_attn, out_0, out_1, out_2
+):
+    nc = tc.nc
+    chunk_order = [chunk for chunks in ROUNDS for chunk in chunks]
+
+    x_rows = x.flatten_outer_dims().rearrange("(p i) k -> p i k", i=TILES)
+    cos_rows = freqs_cos.rearrange("(p i) d -> p i d", i=TILES)
+    sin_rows = freqs_sin.rearrange("(p i) d -> p i d", i=TILES)
+    out_rows = [
+        out.rearrange("b h (p i) d -> p (b h) i d", i=TILES)
+        for out in (out_0, out_1, out_2)
+    ]
+
+    with ExitStack() as ctx:
+        const = ctx.enter_context(tc.tile_pool(name="const", bufs=1))
+        x_in = ctx.enter_context(tc.tile_pool(name="x_in", bufs=TILES // PIECE))
+        w_in = ctx.enter_context(tc.tile_pool(name="w_in", bufs=len(chunk_order)))
+        w_mx = ctx.enter_context(tc.tile_pool(name="w_mx", bufs=len(chunk_order)))
+        stage = ctx.enter_context(tc.tile_pool(name="stage", bufs=2))
+        prods = ctx.enter_context(tc.tile_pool(name="prods", bufs=3))
+        results = ctx.enter_context(tc.tile_pool(name="results", bufs=4))
+        rope_banks = ctx.enter_context(tc.psum_pool(name="rope_banks", bufs=6))
+        side_banks = ctx.enter_context(tc.psum_pool(name="side_banks", bufs=2))
+
+        identity = const.tile([P, P], F32)
+        make_identity(nc, identity[:])
+
+        def load_w_chunk(third, half):
+            w_raw = w_in.tile([P, PASSES, PACK, CHUNK], BF16, tag="w_raw")
+            first = third * C + half * CHUNK
+            for g in range(PASSES):
+                for u in range(2):
+                    k0 = 512 * g + 256 * u
+                    nc.sync.dma_start(
+                        out=w_raw[:, g, 2 * u : 2 * u + 2, :],
+                        in_=w_attn[k0 : k0 + 256, first : first + CHUNK].rearrange(
+                            "(q e) n -> q e n", e=2
+                        ),
+                    )
+            return w_raw
+
+        def load_x_piece(piece):
+            x_raw = x_in.tile([P, PIECE, C], BF16, tag="x_raw")
+            i0 = piece * PIECE
+            nc.sync.dma_start(out=x_raw[:], in_=x_rows[:, i0 : i0 + PIECE, :])
+            return x_raw
+
+        table = const.tile([P, 2, TILES, D], BF16)
+        sin_raw = const.tile([P, TILES, D], BF16)
+
+        w_raws = {chunk_order[0]: load_w_chunk(*chunk_order[0])}
+        x_raws = [load_x_piece(0)]
+        nc.sync.dma_start(out=table[:, 0, :, :], in_=cos_rows)
+        nc.sync.dma_start(out=sin_raw[:], in_=sin_rows)
+        for piece in range(1, TILES // PIECE):
+            x_raws.append(load_x_piece(piece))
+        for chunk in chunk_order[1:]:
+            w_raws[chunk] = load_w_chunk(*chunk)
+
+        nc.gpsimd.tensor_scalar(
+            out=table[:, 1, :, 0:HALF],
+            in0=sin_raw[:, :, HALF:D],
+            scalar1=1.0,
+            scalar2=0.0,
+            op0=MULT,
+            op1=ADD,
+        )
+        nc.gpsimd.tensor_scalar(
+            out=table[:, 1, :, HALF:D],
+            in0=sin_raw[:, :, 0:HALF],
+            scalar1=-1.0,
+            scalar2=0.0,
+            op0=MULT,
+            op1=ADD,
+        )
+
+        w_codes = {}
+        w_scales = {}
+
+        def quantise_w_chunk(chunk, copy):
+            w_grouped = stage.tile(
+                [P, PASSES, CHUNK, PACK], BF16, tag="w_grouped", align_bytes=64
+            )
+            for g in range(PASSES):
+                copy(
+                    out=w_grouped[:, g].rearrange("p (c i) t -> p c t i", i=4),
+                    in_=w_raws[chunk][:, g].rearrange("p t (c i) -> p c t i", i=4),
+                )
+            codes = w_mx.tile([P, PASSES, CHUNK], U32, tag="w_codes", align_bytes=64)
+            scales = w_mx.tile([P, PASSES, CHUNK], U8, tag="w_scales", align_bytes=64)
+            nc.vector.quantize_mx(
+                out=codes[:].rearrange("p g n -> p (g n)").bitcast(FP8X4),
+                scales=scales[:].rearrange("p g n -> p (g n)"),
+                in_=w_grouped[:].rearrange("p g n t -> p (g n t)"),
+            )
+            w_codes[chunk] = codes
+            w_scales[chunk] = scales
+
+        quantise_w_chunk(chunk_order[0], nc.vector.tensor_copy)
+
+        x_codes = const.tile([P, TILES, PASSES, P], U32, align_bytes=64)
+        x_scales = const.tile([P, TILES, PASSES, P], U8, align_bytes=64)
+        for piece in range(TILES // PIECE):
+            x_words = x_raws[piece][:].bitcast(F32)
+            x_grouped = stage.tile(
+                [P, PIECE, PASSES, P, PACK], BF16, tag="x_grouped", align_bytes=64
+            )
+            x_grouped_words = x_grouped[:].bitcast(F32)
+            for j in range(PIECE):
+                flipped = side_banks.tile([P, 2 * PASSES, P], F32, tag="side")
+                for gu in range(2 * PASSES):
+                    nc.tensor.transpose(
+                        flipped[:, gu, :],
+                        x_words[:, j, P * gu : P * (gu + 1)],
+                        identity[:],
+                    )
+                nc.scalar.copy(
+                    out=x_grouped_words[:, j],
+                    in_=flipped[:].rearrange("q (g u) p -> q g p u", u=2),
+                )
+            i0 = piece * PIECE
+            nc.vector.quantize_mx(
+                out=x_codes[:, i0 : i0 + PIECE]
+                .rearrange("q i g p -> q (i g p)")
+                .bitcast(FP8X4),
+                scales=x_scales[:, i0 : i0 + PIECE].rearrange("q i g p -> q (i g p)"),
+                in_=x_grouped[:].rearrange("q i g p t -> q (i g p t)"),
+            )
+
+        for chunk in chunk_order[1:]:
+            quantise_w_chunk(chunk, nc.scalar.copy)
+
+        def project(i, chunk, bank):
+            for g in range(PASSES):
+                nc.tensor.matmul_mx(
+                    out=bank[:],
+                    lhsT=x_codes[:, i, g, :].bitcast(FP8X4),
+                    lhsT_scale=x_scales[:, i, g, :],
+                    rhs=w_codes[chunk][:, g, :].bitcast(FP8X4),
+                    rhs_scale=w_scales[chunk][:, g, :],
+                    start=(g == 0),
+                    stop=(g == PASSES - 1),
+                )
+
+        for chunks in ROUNDS:
+            for i_store in range(0, TILES, STORE_TILES):
+                result = {}
+                for chunk in chunks:
+                    result[chunk] = results.tile(
+                        [P, CHUNK_HEADS, STORE_TILES, D], F32, tag="result", name="result"
+                    )
+                for j0 in range(0, STORE_TILES, PIECE):
+                    for chunk in chunks:
+                        if chunk[0] == V_THIRD:
+                            for j in range(j0, j0 + PIECE):
+                                bank = side_banks.tile([P, CHUNK], F32, tag="side")
+                                project(i_store + j, chunk, bank)
+                                nc.scalar.copy(
+                                    out=result[chunk][:, :, j, :],
+                                    in_=bank[:].rearrange("p (h d) -> p h d", d=D),
+                                )
+                            continue
+                        both = prods.tile([P, PIECE, 2, CHUNK_HEADS, D], F32, tag="both")
+                        for b in range(PIECE):
+                            i = i_store + j0 + b
+                            bank = rope_banks.tile([P, CHUNK], F32, tag="rope")
+                            project(i, chunk, bank)
+                            nc.vector.tensor_tensor(
+                                out=both[:, b],
+                                in0=bank[:]
+                                .rearrange("p (h d) -> p h d", d=D)
+                                .unsqueeze(1)
+                                .to_broadcast([P, 2, CHUNK_HEADS, D]),
+                                in1=table[:, :, i, :]
+                                .unsqueeze(2)
+                                .to_broadcast([P, 2, CHUNK_HEADS, D]),
+                                op=MULT,
+                            )
+                        for side in range(2):
+                            here = slice(side * HALF, (side + 1) * HALF)
+                            there = slice((1 - side) * HALF, (2 - side) * HALF)
+                            nc.gpsimd.tensor_tensor(
+                                out=result[chunk][:, :, j0 : j0 + PIECE, here].rearrange(
+                                    "p h b j -> p b h j"
+                                ),
+                                in0=both[:, :, 0, :, here],
+                                in1=both[:, :, 1, :, there],
+                                op=ADD,
+                            )
+                for third, half in chunks:
+                    h0 = half * CHUNK_HEADS
+                    nc.sync.dma_start(
+                        out=out_rows[third][
+                            :, h0 : h0 + CHUNK_HEADS, i_store : i_store + STORE_TILES, :
+                        ],
+                        in_=result[(third, half)][:],
+                    )

@@ -18,11 +18,14 @@ D = 128
 HALF = D // 2
 TILES = T // P
 PACK = 4
-PASSES = C // (P * PACK)
+K_PASS = P * PACK
+PASSES = C // K_PASS
+PASS_WORDS = K_PASS // 2
 CHUNK = 512
 CHUNK_HEADS = CHUNK // D
 PIECE = 2
 STORE_TILES = 6
+VECTOR_SUM_TILES = 4
 
 FLOPS = 2 * T * C * 3 * C
 
@@ -50,7 +53,7 @@ def tile_swaattention_pa_kernel(
         w_in = ctx.enter_context(tc.tile_pool(name="w_in", bufs=len(chunk_order)))
         w_mx = ctx.enter_context(tc.tile_pool(name="w_mx", bufs=len(chunk_order)))
         stage = ctx.enter_context(tc.tile_pool(name="stage", bufs=2))
-        prods = ctx.enter_context(tc.tile_pool(name="prods", bufs=3))
+        prods = ctx.enter_context(tc.tile_pool(name="prods", bufs=4))
         results = ctx.enter_context(tc.tile_pool(name="results", bufs=4))
         rope_banks = ctx.enter_context(tc.psum_pool(name="rope_banks", bufs=6))
         side_banks = ctx.enter_context(tc.psum_pool(name="side_banks", bufs=2))
@@ -62,14 +65,12 @@ def tile_swaattention_pa_kernel(
             w_raw = w_in.tile([P, PASSES, PACK, CHUNK], BF16, tag="w_raw")
             first = third * C + half * CHUNK
             for g in range(PASSES):
-                for u in range(2):
-                    k0 = 512 * g + 256 * u
-                    nc.sync.dma_start(
-                        out=w_raw[:, g, 2 * u : 2 * u + 2, :],
-                        in_=w_attn[k0 : k0 + 256, first : first + CHUNK].rearrange(
-                            "(q e) n -> q e n", e=2
-                        ),
-                    )
+                nc.sync.dma_start(
+                    out=w_raw[:, g],
+                    in_=w_attn[
+                        K_PASS * g : K_PASS * (g + 1), first : first + CHUNK
+                    ].rearrange("(q t) n -> q t n", t=PACK),
+                )
             return w_raw
 
         def load_x_piece(piece):
@@ -81,8 +82,8 @@ def tile_swaattention_pa_kernel(
         table = const.tile([P, 2, TILES, D], BF16)
         sin_raw = const.tile([P, TILES, D], BF16)
 
-        w_raws = {chunk_order[0]: load_w_chunk(*chunk_order[0])}
         x_raws = [load_x_piece(0)]
+        w_raws = {chunk_order[0]: load_w_chunk(*chunk_order[0])}
         nc.sync.dma_start(out=table[:, 0, :, :], in_=cos_rows)
         nc.sync.dma_start(out=sin_raw[:], in_=sin_rows)
         for piece in range(1, TILES // PIECE):
@@ -114,18 +115,19 @@ def tile_swaattention_pa_kernel(
             w_grouped = stage.tile(
                 [P, PASSES, CHUNK, PACK], BF16, tag="w_grouped", align_bytes=64
             )
+            codes = w_mx.tile([P, PASSES, CHUNK], U32, tag="w_codes", align_bytes=64)
+            scales = w_mx.tile([P, PASSES, CHUNK], U8, tag="w_scales", align_bytes=64)
             for g in range(PASSES):
                 copy(
                     out=w_grouped[:, g].rearrange("p (c i) t -> p c t i", i=4),
                     in_=w_raws[chunk][:, g].rearrange("p t (c i) -> p c t i", i=4),
                 )
-            codes = w_mx.tile([P, PASSES, CHUNK], U32, tag="w_codes", align_bytes=64)
-            scales = w_mx.tile([P, PASSES, CHUNK], U8, tag="w_scales", align_bytes=64)
-            nc.vector.quantize_mx(
-                out=codes[:].rearrange("p g n -> p (g n)").bitcast(FP8X4),
-                scales=scales[:].rearrange("p g n -> p (g n)"),
-                in_=w_grouped[:].rearrange("p g n t -> p (g n t)"),
-            )
+            for g in range(PASSES):
+                nc.vector.quantize_mx(
+                    out=codes[:, g].bitcast(FP8X4),
+                    scales=scales[:, g],
+                    in_=w_grouped[:, g].rearrange("p n t -> p (n t)"),
+                )
             w_codes[chunk] = codes
             w_scales[chunk] = scales
 
@@ -141,12 +143,13 @@ def tile_swaattention_pa_kernel(
             x_grouped_words = x_grouped[:].bitcast(F32)
             for j in range(PIECE):
                 flipped = side_banks.tile([P, 2 * PASSES, P], F32, tag="side")
-                for gu in range(2 * PASSES):
-                    nc.tensor.transpose(
-                        flipped[:, gu, :],
-                        x_words[:, j, P * gu : P * (gu + 1)],
-                        identity[:],
-                    )
+                for g in range(PASSES):
+                    for u in range(2):
+                        nc.tensor.transpose(
+                            flipped[:, 2 * g + u, :],
+                            x_words[:, j, PASS_WORDS * g + u : PASS_WORDS * (g + 1) : 2],
+                            identity[:],
+                        )
                 nc.scalar.copy(
                     out=x_grouped_words[:, j],
                     in_=flipped[:].rearrange("q (g u) p -> q g p u", u=2),
@@ -160,9 +163,6 @@ def tile_swaattention_pa_kernel(
                 in_=x_grouped[:].rearrange("q i g p t -> q (i g p t)"),
             )
 
-        for chunk in chunk_order[1:]:
-            quantise_w_chunk(chunk, nc.scalar.copy)
-
         def project(i, chunk, bank):
             for g in range(PASSES):
                 nc.tensor.matmul_mx(
@@ -175,8 +175,19 @@ def tile_swaattention_pa_kernel(
                     stop=(g == PASSES - 1),
                 )
 
-        for chunks in ROUNDS:
+        def store(chunk, result_tile, i_store, j0, tiles):
+            third, half = chunk
+            h0 = half * CHUNK_HEADS
+            nc.sync.dma_start(
+                out=out_rows[third][
+                    :, h0 : h0 + CHUNK_HEADS, i_store + j0 : i_store + j0 + tiles, :
+                ],
+                in_=result_tile[:, :, j0 : j0 + tiles, :],
+            )
+
+        for r, chunks in enumerate(ROUNDS):
             for i_store in range(0, TILES, STORE_TILES):
+                taper = r == len(ROUNDS) - 1 and i_store + STORE_TILES == TILES
                 result = {}
                 for chunk in chunks:
                     result[chunk] = results.tile(
@@ -209,10 +220,13 @@ def tile_swaattention_pa_kernel(
                                 .to_broadcast([P, 2, CHUNK_HEADS, D]),
                                 op=MULT,
                             )
+                        adder = nc.gpsimd
+                        if taper and j0 + VECTOR_SUM_TILES >= STORE_TILES:
+                            adder = nc.vector
                         for side in range(2):
                             here = slice(side * HALF, (side + 1) * HALF)
                             there = slice((1 - side) * HALF, (2 - side) * HALF)
-                            nc.gpsimd.tensor_tensor(
+                            adder.tensor_tensor(
                                 out=result[chunk][:, :, j0 : j0 + PIECE, here].rearrange(
                                     "p h b j -> p b h j"
                                 ),
@@ -220,11 +234,11 @@ def tile_swaattention_pa_kernel(
                                 in1=both[:, :, 1, :, there],
                                 op=ADD,
                             )
-                for third, half in chunks:
-                    h0 = half * CHUNK_HEADS
-                    nc.sync.dma_start(
-                        out=out_rows[third][
-                            :, h0 : h0 + CHUNK_HEADS, i_store : i_store + STORE_TILES, :
-                        ],
-                        in_=result[(third, half)][:],
-                    )
+                        if taper:
+                            store(chunk, result[chunk], i_store, j0, PIECE)
+                if not taper:
+                    for chunk in chunks:
+                        store(chunk, result[chunk], i_store, 0, STORE_TILES)
+                if i_store == 0 and r + 1 < len(ROUNDS):
+                    for chunk in ROUNDS[r + 1]:
+                        quantise_w_chunk(chunk, nc.scalar.copy)

@@ -23,21 +23,24 @@ PASSES = C // K_PASS
 PASS_WORDS = K_PASS // 2
 CHUNK = 512
 CHUNK_HEADS = CHUNK // D
-PIECE = 2
-STORE_TILES = 6
-VECTOR_SUM_TILES = 4
+PAIR = 2
+ROPE_GROUP = 6
+V_GROUP = 4
 
 FLOPS = 2 * T * C * 3 * C
 
-ROUNDS = (((0, 0),), ((1, 0), (2, 0)), ((0, 1), (2, 1)), ((1, 1),))
-V_THIRD = 2
+ROPE_CHUNKS = ((0, 0), (1, 0), (0, 1), (1, 1))
+V_CHUNKS = ((2, 0), (2, 1))
+CHUNK_ORDER = ((0, 0), (1, 0), (2, 0), (0, 1), (2, 1), (1, 1))
 
 
 def tile_swaattention_pa_kernel(
     tc, x, freqs_cos, freqs_sin, w_attn, out_0, out_1, out_2
 ):
     nc = tc.nc
-    chunk_order = [chunk for chunks in ROUNDS for chunk in chunks]
+    rope_groups = [(chunk, i0) for chunk in ROPE_CHUNKS for i0 in range(0, TILES, ROPE_GROUP)]
+    v_groups = [(chunk, i0) for chunk in V_CHUNKS for i0 in range(0, TILES, V_GROUP)]
+    v_start = len(rope_groups) - len(v_groups)
 
     x_rows = x.flatten_outer_dims().rearrange("(p i) k -> p i k", i=TILES)
     cos_rows = freqs_cos.rearrange("(p i) d -> p i d", i=TILES)
@@ -49,12 +52,12 @@ def tile_swaattention_pa_kernel(
 
     with ExitStack() as ctx:
         const = ctx.enter_context(tc.tile_pool(name="const", bufs=1))
-        x_in = ctx.enter_context(tc.tile_pool(name="x_in", bufs=TILES // PIECE))
-        w_in = ctx.enter_context(tc.tile_pool(name="w_in", bufs=len(chunk_order)))
-        w_mx = ctx.enter_context(tc.tile_pool(name="w_mx", bufs=len(chunk_order)))
+        x_in = ctx.enter_context(tc.tile_pool(name="x_in", bufs=TILES // PAIR))
+        w_in = ctx.enter_context(tc.tile_pool(name="w_in", bufs=4))
+        w_mx = ctx.enter_context(tc.tile_pool(name="w_mx", bufs=len(CHUNK_ORDER)))
         stage = ctx.enter_context(tc.tile_pool(name="stage", bufs=2))
         prods = ctx.enter_context(tc.tile_pool(name="prods", bufs=4))
-        results = ctx.enter_context(tc.tile_pool(name="results", bufs=4))
+        results = ctx.enter_context(tc.tile_pool(name="results", bufs=3))
         rope_banks = ctx.enter_context(tc.psum_pool(name="rope_banks", bufs=6))
         side_banks = ctx.enter_context(tc.psum_pool(name="side_banks", bufs=2))
 
@@ -73,22 +76,22 @@ def tile_swaattention_pa_kernel(
                 )
             return w_raw
 
-        def load_x_piece(piece):
-            x_raw = x_in.tile([P, PIECE, C], BF16, tag="x_raw")
-            i0 = piece * PIECE
-            nc.sync.dma_start(out=x_raw[:], in_=x_rows[:, i0 : i0 + PIECE, :])
+        def load_x_pair(pair):
+            x_raw = x_in.tile([P, PAIR, C], BF16, tag="x_raw")
+            i0 = pair * PAIR
+            nc.sync.dma_start(out=x_raw[:], in_=x_rows[:, i0 : i0 + PAIR, :])
             return x_raw
 
         table = const.tile([P, 2, TILES, D], BF16)
         sin_raw = const.tile([P, TILES, D], BF16)
 
-        x_raws = [load_x_piece(0)]
-        w_raws = {chunk_order[0]: load_w_chunk(*chunk_order[0])}
+        x_raws = [load_x_pair(0)]
+        w_raws = {CHUNK_ORDER[0]: load_w_chunk(*CHUNK_ORDER[0])}
         nc.sync.dma_start(out=table[:, 0, :, :], in_=cos_rows)
         nc.sync.dma_start(out=sin_raw[:], in_=sin_rows)
-        for piece in range(1, TILES // PIECE):
-            x_raws.append(load_x_piece(piece))
-        for chunk in chunk_order[1:]:
+        for pair in range(1, TILES // PAIR):
+            x_raws.append(load_x_pair(pair))
+        for chunk in CHUNK_ORDER[1:]:
             w_raws[chunk] = load_w_chunk(*chunk)
 
         nc.gpsimd.tensor_scalar(
@@ -115,33 +118,32 @@ def tile_swaattention_pa_kernel(
             w_grouped = stage.tile(
                 [P, PASSES, CHUNK, PACK], BF16, tag="w_grouped", align_bytes=64
             )
-            codes = w_mx.tile([P, PASSES, CHUNK], U32, tag="w_codes", align_bytes=64)
-            scales = w_mx.tile([P, PASSES, CHUNK], U8, tag="w_scales", align_bytes=64)
             for g in range(PASSES):
                 copy(
                     out=w_grouped[:, g].rearrange("p (c i) t -> p c t i", i=4),
                     in_=w_raws[chunk][:, g].rearrange("p t (c i) -> p c t i", i=4),
                 )
-            for g in range(PASSES):
-                nc.vector.quantize_mx(
-                    out=codes[:, g].bitcast(FP8X4),
-                    scales=scales[:, g],
-                    in_=w_grouped[:, g].rearrange("p n t -> p (n t)"),
-                )
+            codes = w_mx.tile([P, PASSES, CHUNK], U32, tag="w_codes", align_bytes=64)
+            scales = w_mx.tile([P, PASSES, CHUNK], U8, tag="w_scales", align_bytes=64)
+            nc.vector.quantize_mx(
+                out=codes[:].rearrange("p g n -> p (g n)").bitcast(FP8X4),
+                scales=scales[:].rearrange("p g n -> p (g n)"),
+                in_=w_grouped[:].rearrange("p g n t -> p (g n t)"),
+            )
             w_codes[chunk] = codes
             w_scales[chunk] = scales
 
-        quantise_w_chunk(chunk_order[0], nc.vector.tensor_copy)
+        quantise_w_chunk(CHUNK_ORDER[0], nc.vector.tensor_copy)
 
         x_codes = const.tile([P, TILES, PASSES, P], U32, align_bytes=64)
         x_scales = const.tile([P, TILES, PASSES, P], U8, align_bytes=64)
-        for piece in range(TILES // PIECE):
-            x_words = x_raws[piece][:].bitcast(F32)
+        for pair in range(TILES // PAIR):
+            x_words = x_raws[pair][:].bitcast(F32)
             x_grouped = stage.tile(
-                [P, PIECE, PASSES, P, PACK], BF16, tag="x_grouped", align_bytes=64
+                [P, PAIR, PASSES, P, PACK], BF16, tag="x_grouped", align_bytes=64
             )
             x_grouped_words = x_grouped[:].bitcast(F32)
-            for j in range(PIECE):
+            for j in range(PAIR):
                 flipped = side_banks.tile([P, 2 * PASSES, P], F32, tag="side")
                 for g in range(PASSES):
                     for u in range(2):
@@ -154,14 +156,17 @@ def tile_swaattention_pa_kernel(
                     out=x_grouped_words[:, j],
                     in_=flipped[:].rearrange("q (g u) p -> q g p u", u=2),
                 )
-            i0 = piece * PIECE
+            i0 = pair * PAIR
             nc.vector.quantize_mx(
-                out=x_codes[:, i0 : i0 + PIECE]
+                out=x_codes[:, i0 : i0 + PAIR]
                 .rearrange("q i g p -> q (i g p)")
                 .bitcast(FP8X4),
-                scales=x_scales[:, i0 : i0 + PIECE].rearrange("q i g p -> q (i g p)"),
+                scales=x_scales[:, i0 : i0 + PAIR].rearrange("q i g p -> q (i g p)"),
                 in_=x_grouped[:].rearrange("q i g p t -> q (i g p t)"),
             )
+
+        for chunk in CHUNK_ORDER[1:]:
+            quantise_w_chunk(chunk, nc.scalar.copy)
 
         def project(i, chunk, bank):
             for g in range(PASSES):
@@ -175,70 +180,62 @@ def tile_swaattention_pa_kernel(
                     stop=(g == PASSES - 1),
                 )
 
-        def store(chunk, result_tile, i_store, j0, tiles):
+        def store(chunk, result, i0, j0, tiles):
             third, half = chunk
             h0 = half * CHUNK_HEADS
             nc.sync.dma_start(
                 out=out_rows[third][
-                    :, h0 : h0 + CHUNK_HEADS, i_store + j0 : i_store + j0 + tiles, :
+                    :, h0 : h0 + CHUNK_HEADS, i0 + j0 : i0 + j0 + tiles, :
                 ],
-                in_=result_tile[:, :, j0 : j0 + tiles, :],
+                in_=result[:, :, j0 : j0 + tiles, :],
             )
 
-        for r, chunks in enumerate(ROUNDS):
-            for i_store in range(0, TILES, STORE_TILES):
-                taper = r == len(ROUNDS) - 1 and i_store + STORE_TILES == TILES
-                result = {}
-                for chunk in chunks:
-                    result[chunk] = results.tile(
-                        [P, CHUNK_HEADS, STORE_TILES, D], F32, tag="result", name="result"
-                    )
-                for j0 in range(0, STORE_TILES, PIECE):
-                    for chunk in chunks:
-                        if chunk[0] == V_THIRD:
-                            for j in range(j0, j0 + PIECE):
-                                bank = side_banks.tile([P, CHUNK], F32, tag="side")
-                                project(i_store + j, chunk, bank)
-                                nc.scalar.copy(
-                                    out=result[chunk][:, :, j, :],
-                                    in_=bank[:].rearrange("p (h d) -> p h d", d=D),
-                                )
-                            continue
-                        both = prods.tile([P, PIECE, 2, CHUNK_HEADS, D], F32, tag="both")
-                        for b in range(PIECE):
-                            i = i_store + j0 + b
-                            bank = rope_banks.tile([P, CHUNK], F32, tag="rope")
-                            project(i, chunk, bank)
-                            nc.vector.tensor_tensor(
-                                out=both[:, b],
-                                in0=bank[:]
-                                .rearrange("p (h d) -> p h d", d=D)
-                                .unsqueeze(1)
-                                .to_broadcast([P, 2, CHUNK_HEADS, D]),
-                                in1=table[:, :, i, :]
-                                .unsqueeze(2)
-                                .to_broadcast([P, 2, CHUNK_HEADS, D]),
-                                op=MULT,
-                            )
-                        adder = nc.gpsimd
-                        if taper and j0 + VECTOR_SUM_TILES >= STORE_TILES:
-                            adder = nc.vector
-                        for side in range(2):
-                            here = slice(side * HALF, (side + 1) * HALF)
-                            there = slice((1 - side) * HALF, (2 - side) * HALF)
-                            adder.tensor_tensor(
-                                out=result[chunk][:, :, j0 : j0 + PIECE, here].rearrange(
-                                    "p h b j -> p b h j"
-                                ),
-                                in0=both[:, :, 0, :, here],
-                                in1=both[:, :, 1, :, there],
-                                op=ADD,
-                            )
-                        if taper:
-                            store(chunk, result[chunk], i_store, j0, PIECE)
-                if not taper:
-                    for chunk in chunks:
-                        store(chunk, result[chunk], i_store, 0, STORE_TILES)
-                if i_store == 0 and r + 1 < len(ROUNDS):
-                    for chunk in ROUNDS[r + 1]:
-                        quantise_w_chunk(chunk, nc.scalar.copy)
+        def rotate_pair(chunk, i0, j0, rotated):
+            both = prods.tile([P, PAIR, 2, CHUNK_HEADS, D], F32, tag="both")
+            for b in range(PAIR):
+                i = i0 + j0 + b
+                bank = rope_banks.tile([P, CHUNK], F32, tag="rope")
+                project(i, chunk, bank)
+                nc.vector.tensor_tensor(
+                    out=both[:, b],
+                    in0=bank[:]
+                    .rearrange("p (h d) -> p h d", d=D)
+                    .unsqueeze(1)
+                    .to_broadcast([P, 2, CHUNK_HEADS, D]),
+                    in1=table[:, :, i, :].unsqueeze(2).to_broadcast([P, 2, CHUNK_HEADS, D]),
+                    op=MULT,
+                )
+            for side in range(2):
+                here = slice(side * HALF, (side + 1) * HALF)
+                there = slice((1 - side) * HALF, (2 - side) * HALF)
+                nc.gpsimd.tensor_tensor(
+                    out=rotated[:, :, j0 : j0 + PAIR, here].rearrange("p h b j -> p b h j"),
+                    in0=both[:, :, 0, :, here],
+                    in1=both[:, :, 1, :, there],
+                    op=ADD,
+                )
+
+        def copy_pair(chunk, i0, j0, plain):
+            for j in range(j0, j0 + PAIR):
+                bank = side_banks.tile([P, CHUNK], F32, tag="side")
+                project(i0 + j, chunk, bank)
+                nc.scalar.copy(
+                    out=plain[:, :, j, :], in_=bank[:].rearrange("p (h d) -> p h d", d=D)
+                )
+
+        for s, (rope_chunk, rope_i0) in enumerate(rope_groups):
+            last = s == len(rope_groups) - 1
+            rotated = results.tile([P, CHUNK_HEADS, ROPE_GROUP, D], F32, tag="rotated")
+            if s >= v_start:
+                v_chunk, v_i0 = v_groups[s - v_start]
+                plain = results.tile([P, CHUNK_HEADS, V_GROUP, D], F32, tag="plain")
+            for j0 in range(0, ROPE_GROUP, PAIR):
+                rotate_pair(rope_chunk, rope_i0, j0, rotated)
+                if last:
+                    store(rope_chunk, rotated, rope_i0, j0, PAIR)
+                if s >= v_start and j0 < V_GROUP:
+                    copy_pair(v_chunk, v_i0, j0, plain)
+                    if j0 + PAIR == V_GROUP:
+                        store(v_chunk, plain, v_i0, 0, V_GROUP)
+            if not last:
+                store(rope_chunk, rotated, rope_i0, 0, ROPE_GROUP)

@@ -183,7 +183,8 @@ def tile_swaattention_pa_kernel(
         def store(chunk, result, i0, j0, tiles):
             third, half = chunk
             h0 = half * CHUNK_HEADS
-            nc.sync.dma_start(
+            queue = nc.scalar if third == 2 else nc.sync
+            queue.dma_start(
                 out=out_rows[third][
                     :, h0 : h0 + CHUNK_HEADS, i0 + j0 : i0 + j0 + tiles, :
                 ],

@@ -52,11 +52,11 @@ def tile_swaattention_pa_kernel(
 
     with ExitStack() as ctx:
         const = ctx.enter_context(tc.tile_pool(name="const", bufs=1))
-        x_in = ctx.enter_context(tc.tile_pool(name="x_in", bufs=TILES // PAIR))
+        x_in = ctx.enter_context(tc.tile_pool(name="x_in", bufs=4))
         w_in = ctx.enter_context(tc.tile_pool(name="w_in", bufs=4))
         w_mx = ctx.enter_context(tc.tile_pool(name="w_mx", bufs=len(CHUNK_ORDER)))
         stage = ctx.enter_context(tc.tile_pool(name="stage", bufs=2))
-        prods = ctx.enter_context(tc.tile_pool(name="prods", bufs=4))
+        prods = ctx.enter_context(tc.tile_pool(name="prods", bufs=6))
         results = ctx.enter_context(tc.tile_pool(name="results", bufs=3))
         rope_banks = ctx.enter_context(tc.psum_pool(name="rope_banks", bufs=6))
         side_banks = ctx.enter_context(tc.psum_pool(name="side_banks", bufs=2))
@@ -87,8 +87,8 @@ def tile_swaattention_pa_kernel(
 
         x_raws = [load_x_pair(0)]
         w_raws = {CHUNK_ORDER[0]: load_w_chunk(*CHUNK_ORDER[0])}
-        nc.sync.dma_start(out=table[:, 0, :, :], in_=cos_rows)
         nc.sync.dma_start(out=sin_raw[:], in_=sin_rows)
+        nc.sync.dma_start(out=table[:, 0, :, :], in_=cos_rows)
         for pair in range(1, TILES // PAIR):
             x_raws.append(load_x_pair(pair))
         for chunk in CHUNK_ORDER[1:]:
@@ -114,26 +114,34 @@ def tile_swaattention_pa_kernel(
         w_codes = {}
         w_scales = {}
 
-        def quantise_w_chunk(chunk, copy):
+        def quantise_w_chunk(chunk, copies, by_pass):
             w_grouped = stage.tile(
                 [P, PASSES, CHUNK, PACK], BF16, tag="w_grouped", align_bytes=64
             )
             for g in range(PASSES):
-                copy(
+                copies[g](
                     out=w_grouped[:, g].rearrange("p (c i) t -> p c t i", i=4),
                     in_=w_raws[chunk][:, g].rearrange("p t (c i) -> p c t i", i=4),
                 )
             codes = w_mx.tile([P, PASSES, CHUNK], U32, tag="w_codes", align_bytes=64)
             scales = w_mx.tile([P, PASSES, CHUNK], U8, tag="w_scales", align_bytes=64)
-            nc.vector.quantize_mx(
-                out=codes[:].rearrange("p g n -> p (g n)").bitcast(FP8X4),
-                scales=scales[:].rearrange("p g n -> p (g n)"),
-                in_=w_grouped[:].rearrange("p g n t -> p (g n t)"),
-            )
+            if by_pass:
+                for g in range(PASSES):
+                    nc.vector.quantize_mx(
+                        out=codes[:, g].bitcast(FP8X4),
+                        scales=scales[:, g],
+                        in_=w_grouped[:, g].rearrange("p n t -> p (n t)"),
+                    )
+            else:
+                nc.vector.quantize_mx(
+                    out=codes[:].rearrange("p g n -> p (g n)").bitcast(FP8X4),
+                    scales=scales[:].rearrange("p g n -> p (g n)"),
+                    in_=w_grouped[:].rearrange("p g n t -> p (g n t)"),
+                )
             w_codes[chunk] = codes
             w_scales[chunk] = scales
 
-        quantise_w_chunk(CHUNK_ORDER[0], nc.vector.tensor_copy)
+        quantise_w_chunk(CHUNK_ORDER[0], (nc.vector.tensor_copy, nc.scalar.copy), True)
 
         x_codes = const.tile([P, TILES, PASSES, P], U32, align_bytes=64)
         x_scales = const.tile([P, TILES, PASSES, P], U8, align_bytes=64)
@@ -166,7 +174,7 @@ def tile_swaattention_pa_kernel(
             )
 
         for chunk in CHUNK_ORDER[1:]:
-            quantise_w_chunk(chunk, nc.scalar.copy)
+            quantise_w_chunk(chunk, (nc.scalar.copy, nc.scalar.copy), False)
 
         def project(i, chunk, bank):
             for g in range(PASSES):
@@ -180,10 +188,9 @@ def tile_swaattention_pa_kernel(
                     stop=(g == PASSES - 1),
                 )
 
-        def store(chunk, result, i0, j0, tiles):
+        def store(chunk, result, i0, j0, tiles, queue):
             third, half = chunk
             h0 = half * CHUNK_HEADS
-            queue = nc.scalar if third == 2 else nc.sync
             queue.dma_start(
                 out=out_rows[third][
                     :, h0 : h0 + CHUNK_HEADS, i0 + j0 : i0 + j0 + tiles, :
@@ -191,7 +198,7 @@ def tile_swaattention_pa_kernel(
                 in_=result[:, :, j0 : j0 + tiles, :],
             )
 
-        def rotate_pair(chunk, i0, j0, rotated):
+        def multiply_pair(chunk, i0, j0):
             both = prods.tile([P, PAIR, 2, CHUNK_HEADS, D], F32, tag="both")
             for b in range(PAIR):
                 i = i0 + j0 + b
@@ -206,10 +213,13 @@ def tile_swaattention_pa_kernel(
                     in1=table[:, :, i, :].unsqueeze(2).to_broadcast([P, 2, CHUNK_HEADS, D]),
                     op=MULT,
                 )
+            return both
+
+        def add_pair(adder, both, j0, rotated):
             for side in range(2):
                 here = slice(side * HALF, (side + 1) * HALF)
                 there = slice((1 - side) * HALF, (2 - side) * HALF)
-                nc.gpsimd.tensor_tensor(
+                adder.tensor_tensor(
                     out=rotated[:, :, j0 : j0 + PAIR, here].rearrange("p h b j -> p b h j"),
                     in0=both[:, :, 0, :, here],
                     in1=both[:, :, 1, :, there],
@@ -230,13 +240,21 @@ def tile_swaattention_pa_kernel(
             if s >= v_start:
                 v_chunk, v_i0 = v_groups[s - v_start]
                 plain = results.tile([P, CHUNK_HEADS, V_GROUP, D], F32, tag="plain")
+            kept = []
             for j0 in range(0, ROPE_GROUP, PAIR):
-                rotate_pair(rope_chunk, rope_i0, j0, rotated)
+                both = multiply_pair(rope_chunk, rope_i0, j0)
                 if last:
-                    store(rope_chunk, rotated, rope_i0, j0, PAIR)
+                    kept.append((both, j0))
+                else:
+                    add_pair(nc.gpsimd, both, j0, rotated)
+                    if s == len(rope_groups) - 2:
+                        store(rope_chunk, rotated, rope_i0, j0, PAIR, nc.sync)
                 if s >= v_start and j0 < V_GROUP:
                     copy_pair(v_chunk, v_i0, j0, plain)
                     if j0 + PAIR == V_GROUP:
-                        store(v_chunk, plain, v_i0, 0, V_GROUP)
-            if not last:
-                store(rope_chunk, rotated, rope_i0, 0, ROPE_GROUP)
+                        store(v_chunk, plain, v_i0, 0, V_GROUP, nc.scalar)
+            if s < len(rope_groups) - 2:
+                store(rope_chunk, rotated, rope_i0, 0, ROPE_GROUP, nc.sync)
+            for both, j0 in kept:
+                add_pair(nc.vector, both, j0, rotated)
+                store(rope_chunk, rotated, rope_i0, j0, PAIR, nc.scalar)

from contextlib import ExitStack

import concourse.mybir as mybir
from concourse.masks import make_identity

BF16 = mybir.dt.bfloat16
F32 = mybir.dt.float32
U32 = mybir.dt.uint32
U8 = mybir.dt.uint8
FP8X4 = mybir.dt.float8_e4m3fn_x4
MULT = mybir.AluOpType.mult
ADD = mybir.AluOpType.add

P = 128
T = 1536
C = 1024
D = 128
HALF = D // 2
TILES = T // P
PACK = 4
K_PASS = P * PACK
PASSES = C // K_PASS
PASS_WORDS = K_PASS // 2
CHUNK = 512
CHUNK_HEADS = CHUNK // D
PAIR = 2
ROPE_GROUP = 6
V_GROUP = 4

FLOPS = 2 * T * C * 3 * C

ROPE_CHUNKS = ((0, 0), (1, 0), (0, 1), (1, 1))
V_CHUNKS = ((2, 0), (2, 1))
CHUNK_ORDER = ((0, 0), (1, 0), (2, 0), (0, 1), (2, 1), (1, 1))


def tile_swaattention_pa_kernel(
    tc, x, freqs_cos, freqs_sin, w_attn, out_0, out_1, out_2
):
    nc = tc.nc
    rope_groups = [(chunk, i0) for chunk in ROPE_CHUNKS for i0 in range(0, TILES, ROPE_GROUP)]
    v_groups = [(chunk, i0) for chunk in V_CHUNKS for i0 in range(0, TILES, V_GROUP)]
    v_start = len(rope_groups) - len(v_groups)

    x_rows = x.flatten_outer_dims().rearrange("(p i) k -> p i k", i=TILES)
    cos_rows = freqs_cos.rearrange("(p i) d -> p i d", i=TILES)
    sin_rows = freqs_sin.rearrange("(p i) d -> p i d", i=TILES)
    out_rows = [
        out.rearrange("b h (p i) d -> p (b h) i d", i=TILES)
        for out in (out_0, out_1, out_2)
    ]

    with ExitStack() as ctx:
        const = ctx.enter_context(tc.tile_pool(name="const", bufs=1))
        x_in = ctx.enter_context(tc.tile_pool(name="x_in", bufs=4))
        w_in = ctx.enter_context(tc.tile_pool(name="w_in", bufs=4))
        w_mx = ctx.enter_context(tc.tile_pool(name="w_mx", bufs=len(CHUNK_ORDER)))
        stage = ctx.enter_context(tc.tile_pool(name="stage", bufs=2))
        prods = ctx.enter_context(tc.tile_pool(name="prods", bufs=6))
        results = ctx.enter_context(tc.tile_pool(name="results", bufs=3))
        rope_banks = ctx.enter_context(tc.psum_pool(name="rope_banks", bufs=6))
        side_banks = ctx.enter_context(tc.psum_pool(name="side_banks", bufs=2))

        identity = const.tile([P, P], F32)
        make_identity(nc, identity[:])

        def load_w_chunk(third, half):
            w_raw = w_in.tile([P, PASSES, PACK, CHUNK], BF16, tag="w_raw")
            first = third * C + half * CHUNK
            for g in range(PASSES):
                nc.sync.dma_start(
                    out=w_raw[:, g],
                    in_=w_attn[
                        K_PASS * g : K_PASS * (g + 1), first : first + CHUNK
                    ].rearrange("(q t) n -> q t n", t=PACK),
                )
            return w_raw

        def load_x_pair(pair):
            x_raw = x_in.tile([P, PAIR, C], BF16, tag="x_raw")
            i0 = pair * PAIR
            nc.sync.dma_start(out=x_raw[:], in_=x_rows[:, i0 : i0 + PAIR, :])
            return x_raw

        table = const.tile([P, 2, TILES, D], BF16)
        sin_raw = const.tile([P, TILES, D], BF16)

        x_raws = [load_x_pair(0)]
        w_raws = {CHUNK_ORDER[0]: load_w_chunk(*CHUNK_ORDER[0])}
        nc.sync.dma_start(out=sin_raw[:], in_=sin_rows)
        nc.sync.dma_start(out=table[:, 0, :, :], in_=cos_rows)
        for pair in range(1, TILES // PAIR):
            x_raws.append(load_x_pair(pair))
        for chunk in CHUNK_ORDER[1:]:
            w_raws[chunk] = load_w_chunk(*chunk)

        nc.gpsimd.tensor_scalar(
            out=table[:, 1, :, 0:HALF],
            in0=sin_raw[:, :, HALF:D],
            scalar1=1.0,
            scalar2=0.0,
            op0=MULT,
            op1=ADD,
        )
        nc.gpsimd.tensor_scalar(
            out=table[:, 1, :, HALF:D],
            in0=sin_raw[:, :, 0:HALF],
            scalar1=-1.0,
            scalar2=0.0,
            op0=MULT,
            op1=ADD,
        )

        w_codes = {}
        w_scales = {}

        def quantise_w_chunk(chunk, copies, by_pass):
            w_grouped = stage.tile(
                [P, PASSES, CHUNK, PACK], BF16, tag="w_grouped", align_bytes=64
            )
            for g in range(PASSES):
                copies[g](
                    out=w_grouped[:, g].rearrange("p (c i) t -> p c t i", i=4),
                    in_=w_raws[chunk][:, g].rearrange("p t (c i) -> p c t i", i=4),
                )
            codes = w_mx.tile([P, PASSES, CHUNK], U32, tag="w_codes", align_bytes=64)
            scales = w_mx.tile([P, PASSES, CHUNK], U8, tag="w_scales", align_bytes=64)
            if by_pass:
                for g in range(PASSES):
                    nc.vector.quantize_mx(
                        out=codes[:, g].bitcast(FP8X4),
                        scales=scales[:, g],
                        in_=w_grouped[:, g].rearrange("p n t -> p (n t)"),
                    )
            else:
                nc.vector.quantize_mx(
                    out=codes[:].rearrange("p g n -> p (g n)").bitcast(FP8X4),
                    scales=scales[:].rearrange("p g n -> p (g n)"),
                    in_=w_grouped[:].rearrange("p g n t -> p (g n t)"),
                )
            w_codes[chunk] = codes
            w_scales[chunk] = scales

        quantise_w_chunk(CHUNK_ORDER[0], (nc.vector.tensor_copy, nc.scalar.copy), True)

        x_codes = const.tile([P, TILES, PASSES, P], U32, align_bytes=64)
        x_scales = const.tile([P, TILES, PASSES, P], U8, align_bytes=64)
        for pair in range(TILES // PAIR):
            x_words = x_raws[pair][:].bitcast(F32)
            x_grouped = stage.tile(
                [P, PAIR, PASSES, P, PACK], BF16, tag="x_grouped", align_bytes=64
            )
            x_grouped_words = x_grouped[:].bitcast(F32)
            for j in range(PAIR):
                flipped = side_banks.tile([P, 2 * PASSES, P], F32, tag="side")
                for g in range(PASSES):
                    for u in range(2):
                        nc.tensor.transpose(
                            flipped[:, 2 * g + u, :],
                            x_words[:, j, PASS_WORDS * g + u : PASS_WORDS * (g + 1) : 2],
                            identity[:],
                        )
                nc.scalar.copy(
                    out=x_grouped_words[:, j],
                    in_=flipped[:].rearrange("q (g u) p -> q g p u", u=2),
                )
            i0 = pair * PAIR
            nc.vector.quantize_mx(
                out=x_codes[:, i0 : i0 + PAIR]
                .rearrange("q i g p -> q (i g p)")
                .bitcast(FP8X4),
                scales=x_scales[:, i0 : i0 + PAIR].rearrange("q i g p -> q (i g p)"),
                in_=x_grouped[:].rearrange("q i g p t -> q (i g p t)"),
            )

        for chunk in CHUNK_ORDER[1:]:
            quantise_w_chunk(chunk, (nc.scalar.copy, nc.scalar.copy), False)

        def project(i, chunk, bank):
            for g in range(PASSES):
                nc.tensor.matmul_mx(
                    out=bank[:],
                    lhsT=x_codes[:, i, g, :].bitcast(FP8X4),
                    lhsT_scale=x_scales[:, i, g, :],
                    rhs=w_codes[chunk][:, g, :].bitcast(FP8X4),
                    rhs_scale=w_scales[chunk][:, g, :],
                    start=(g == 0),
                    stop=(g == PASSES - 1),
                )

        def store(chunk, result, i0, j0, tiles, queue):
            third, half = chunk
            h0 = half * CHUNK_HEADS
            queue.dma_start(
                out=out_rows[third][
                    :, h0 : h0 + CHUNK_HEADS, i0 + j0 : i0 + j0 + tiles, :
                ],
                in_=result[:, :, j0 : j0 + tiles, :],
            )

        def multiply_pair(chunk, i0, j0):
            both = prods.tile([P, PAIR, 2, CHUNK_HEADS, D], F32, tag="both")
            for b in range(PAIR):
                i = i0 + j0 + b
                bank = rope_banks.tile([P, CHUNK], F32, tag="rope")
                project(i, chunk, bank)
                nc.vector.tensor_tensor(
                    out=both[:, b],
                    in0=bank[:]
                    .rearrange("p (h d) -> p h d", d=D)
                    .unsqueeze(1)
                    .to_broadcast([P, 2, CHUNK_HEADS, D]),
                    in1=table[:, :, i, :].unsqueeze(2).to_broadcast([P, 2, CHUNK_HEADS, D]),
                    op=MULT,
                )
            return both

        def add_pair(adder, both, j0, rotated):
            for side in range(2):
                here = slice(side * HALF, (side + 1) * HALF)
                there = slice((1 - side) * HALF, (2 - side) * HALF)
                adder.tensor_tensor(
                    out=rotated[:, :, j0 : j0 + PAIR, here].rearrange("p h b j -> p b h j"),
                    in0=both[:, :, 0, :, here],
                    in1=both[:, :, 1, :, there],
                    op=ADD,
                )

        def copy_pair(chunk, i0, j0, plain):
            for j in range(j0, j0 + PAIR):
                bank = side_banks.tile([P, CHUNK], F32, tag="side")
                project(i0 + j, chunk, bank)
                nc.scalar.copy(
                    out=plain[:, :, j, :], in_=bank[:].rearrange("p (h d) -> p h d", d=D)
                )

        for s, (rope_chunk, rope_i0) in enumerate(rope_groups):
            last = s == len(rope_groups) - 1
            rotated = results.tile([P, CHUNK_HEADS, ROPE_GROUP, D], F32, tag="rotated")
            if s >= v_start:
                v_chunk, v_i0 = v_groups[s - v_start]
                plain = results.tile([P, CHUNK_HEADS, V_GROUP, D], F32, tag="plain")
            kept = []
            for j0 in range(0, ROPE_GROUP, PAIR):
                both = multiply_pair(rope_chunk, rope_i0, j0)
                if last:
                    kept.append((both, j0))
                else:
                    add_pair(nc.gpsimd, both, j0, rotated)
                    if s == len(rope_groups) - 2:
                        store(rope_chunk, rotated, rope_i0, j0, PAIR, nc.sync)
                if s >= v_start and j0 < V_GROUP:
                    copy_pair(v_chunk, v_i0, j0, plain)
                    if j0 + PAIR == V_GROUP:
                        store(v_chunk, plain, v_i0, 0, V_GROUP, nc.scalar)
            if s < len(rope_groups) - 2:
                store(rope_chunk, rotated, rope_i0, 0, ROPE_GROUP, nc.sync)
            for both, j0 in kept:
                add_pair(nc.vector, both, j0, rotated)
                store(rope_chunk, rotated, rope_i0, j0, PAIR, nc.scalar)
